import numpy as np
import ml_dtypes


def mxq(x, axis, fmt="e4m3"):
    dtype, down = {"e4m3": (ml_dtypes.float8_e4m3fn, 7), "e5m2": (ml_dtypes.float8_e5m2, 14)}[fmt]
    v = np.moveaxis(np.asarray(x, np.float32).astype(ml_dtypes.bfloat16).astype(np.float64), axis, -1)
    blocks = v.reshape(v.shape[:-1] + (-1, 32))
    amax = np.abs(blocks).max(-1, keepdims=True)
    byte = np.maximum(np.where(amax > 0, np.frexp(amax)[1] - 1 + 127, 0) - down, 1)
    scale = np.exp2(byte - 127.0)
    codes = (blocks / scale).astype(np.float32).astype(dtype).astype(np.float64)
    return np.moveaxis((codes * scale).reshape(v.shape), -1, axis)


WIDE = False


def mx_kscale(k):
    if not WIDE:
        return np.ones(k)
    levels = np.array([10, -10, 5, -5, 0])
    a = np.random.permutation(np.resize(levels, k // 512 * 4)).reshape(k // 512, 4)
    idx = np.arange(k)
    return np.exp2(a[idx // 512, idx % 128 // 32])


BF16 = ml_dtypes.bfloat16


def bf(x):
    return np.asarray(x, np.float32).astype(BF16)


def f64(x):
    return np.asarray(x).astype(np.float64)


B, S, E, H, D, F = 2, 256, 1024, 8, 128, 4096
EPS = 1e-6
QUIET = 3e-5
GELU_C = 0.7978845608028654
HD = H * D


def rmsnorm(x, scale):
    ms = np.mean(np.square(x), axis=-1, keepdims=True)
    return x * (1.0 / np.sqrt(ms + EPS)) * scale


def gelu_tanh(v):
    return 0.5 * v * (1.0 + np.tanh(GELU_C * (v + 0.044715 * v**3)))


def setup_inputs():
    s, t = mx_kscale(HD), mx_kscale(E)
    amp = np.where(np.random.random((B, S, 1)) < 0.125, QUIET, 1.0)
    return {"attn": bf(np.random.standard_normal((B, S, H, D)) * 0.25 * amp[..., None] * s.reshape(H, D)),
            "x": bf(np.random.standard_normal((B, S, E)) * amp),
            "w_out": bf(np.random.standard_normal((H, D, E)) * 1.5 / np.sqrt(HD) / s.reshape(H, D, 1)),
            "scale2": bf(np.random.standard_normal(E) * t),
            "w_gate": bf(np.random.standard_normal((E, F)) / np.sqrt(E) / t[:, None]),
            "w_up": bf(np.random.standard_normal((E, F)) / np.sqrt(E) / t[:, None])}


def reference(attn, x, w_out, scale2, w_gate, w_up):
    a = f64(attn).reshape(B * S, HD)
    h = f64(x).reshape(B * S, E) + (mxq(a, 1, "e4m3") @ mxq(f64(w_out).reshape(HD, E), 0, "e4m3"))
    hq = mxq(rmsnorm(h, f64(scale2)), 1, "e4m3")
    act = gelu_tanh(hq @ mxq(f64(w_gate), 0, "e4m3")) * (hq @ mxq(f64(w_up), 0, "e4m3"))
    return h.reshape(B, S, E), act.reshape(B, S, F)

@@ -1,0 +1,212 @@
+from contextlib import ExitStack
+
+import concourse.mybir as mybir
+from concourse.masks import make_identity
+
+F32 = mybir.dt.float32
+BF16 = mybir.dt.bfloat16
+U32 = mybir.dt.uint32
+U8 = mybir.dt.uint8
+FP8X4 = mybir.dt.float8_e4m3fn_x4
+ACT = mybir.ActivationFunctionType
+ALU = mybir.AluOpType
+
+P = 128
+PACK = 4
+K_PASS = P * PACK
+TOKENS = 512
+E = 1024
+F = 4096
+M_TILES = TOKENS // P
+PASSES = E // K_PASS
+N_TILE = 512
+LOAD_COLS = 1024
+EPS = 1e-6
+
+FLOPS = 2 * TOKENS * E * (E + 2 * F)
+
+
+def regroup(copy, grouped, rows):
+    copy(
+        out=grouped.rearrange("p (c i) t -> p c t i", i=4),
+        in_=rows.rearrange("p t (c i) -> p c t i", i=4),
+    )
+
+
+def tile_block_pb_kernel(tc, attn, x, w_out, scale2, w_gate, w_up, out_0, out_1):
+    nc = tc.nc
+    attn_rows = attn.rearrange("b s i d -> (b s) (i d)")
+    x_rows = x.rearrange("b s e -> (b s) e")
+    w_out_rows = w_out.rearrange("i d e -> (i d) e")
+    h_rows = out_0.rearrange("b s e -> (b s) e")
+    act_rows = out_1.rearrange("b s f -> (b s) f")
+    gate_rows = w_gate.rearrange("(g t p) n -> g p t n", t=PACK, p=P)
+    up_rows = w_up.rearrange("(g t p) n -> g p t n", t=PACK, p=P)
+
+    with ExitStack() as ctx:
+        const = ctx.enter_context(tc.tile_pool(name="const", bufs=1))
+        keep = ctx.enter_context(tc.tile_pool(name="keep", bufs=1))
+        raw_pool = ctx.enter_context(tc.tile_pool(name="raw", bufs=8))
+        stage = ctx.enter_context(tc.tile_pool(name="stage", bufs=3))
+        code_pool = ctx.enter_context(tc.tile_pool(name="codes", bufs=3))
+        work = ctx.enter_context(tc.tile_pool(name="work", bufs=3))
+        psum = ctx.enter_context(tc.psum_pool(name="psum", bufs=8))
+
+        ident_f32 = const.tile([P, P], F32)
+        make_identity(nc, ident_f32[:])
+        ident_bf16 = const.tile([P, P], BF16)
+        make_identity(nc, ident_bf16[:])
+        ones = const.tile([P, P], BF16)
+        nc.vector.memset(ones[:], 1.0)
+        eps = const.tile([P, 1], F32)
+        nc.vector.memset(eps[:], EPS)
+        gain_row = const.tile([P, E], BF16)
+        nc.vector.memset(gain_row[:], 0.0)
+        nc.scalar.dma_start(out=gain_row[0:1, :], in_=scale2.unsqueeze(0))
+
+        a_sb = keep.tile([P, M_TILES, E], BF16)
+        for m in range(M_TILES):
+            nc.sync.dma_start(out=a_sb[:, m, :], in_=attn_rows[m * P : (m + 1) * P, :])
+        w_out_raw = []
+        for g in range(PASSES):
+            raw = raw_pool.tile([P, PACK, LOAD_COLS], BF16, tag="raw", name="raw_o")
+            for u in range(2):
+                first = g * K_PASS + u * 2 * P
+                nc.sync.dma_start(
+                    out=raw[:, 2 * u : 2 * u + 2, :],
+                    in_=w_out_rows[first : first + 2 * P, :].rearrange("(p e) n -> p e n", e=2),
+                )
+            w_out_raw.append(raw)
+        x_sb = keep.tile([P, M_TILES, E], BF16)
+        nc.sync.dma_start(out=x_sb[:], in_=x_rows.rearrange("(m p) e -> p m e", p=P))
+
+        gain = const.tile([P, E], F32)
+        for n in range(E // N_TILE):
+            cols = slice(n * N_TILE, (n + 1) * N_TILE)
+            spread = psum.tile([P, N_TILE], F32, tag="bank", name="spread")
+            nc.tensor.matmul(out=spread[:], lhsT=ones[:], rhs=gain_row[:, cols], start=True, stop=True)
+            nc.scalar.copy(out=gain[:, cols], in_=spread[:])
+
+        a_grouped = keep.tile([P, M_TILES, PASSES * P * PACK], BF16, align_bytes=64)
+        a_codes = keep.tile([P, M_TILES, PASSES, P], U32, align_bytes=64)
+        a_scales = keep.tile([P, M_TILES, PASSES, P], U8, align_bytes=64)
+        for m in range(M_TILES):
+            a_words = a_sb[:, m, :].bitcast(F32)
+            a_t = psum.tile([P, PASSES, 2, P], F32, tag="bank", name="a_t")
+            for g in range(PASSES):
+                for u in range(2):
+                    w0 = (2 * g + u) * P
+                    nc.tensor.transpose(a_t[:, g, u, :], a_words[:, w0 : w0 + P], ident_f32[:])
+            nc.scalar.copy(
+                out=a_grouped[:, m, :].bitcast(F32).rearrange("p (g r u) -> p g r u", g=PASSES, u=2),
+                in_=a_t[:].rearrange("p g u r -> p g r u"),
+            )
+            nc.vector.quantize_mx(
+                out=a_codes[:, m].rearrange("p g r -> p (g r)").bitcast(FP8X4),
+                scales=a_scales[:, m].rearrange("p g r -> p (g r)"),
+                in_=a_grouped[:, m, :],
+            )
+
+        wo_codes = keep.tile([P, PASSES, E], U32, align_bytes=64)
+        wo_scales = keep.tile([P, PASSES, E], U8, align_bytes=64)
+        for g in range(PASSES):
+            grouped = stage.tile([P, 2, N_TILE, PACK], BF16, align_bytes=64, tag="grouped", name="grouped")
+            regroup(nc.vector.tensor_copy, grouped[:, 0], w_out_raw[g][:, :, 0:N_TILE])
+            regroup(nc.scalar.copy, grouped[:, 1], w_out_raw[g][:, :, N_TILE : 2 * N_TILE])
+            nc.vector.quantize_mx(
+                out=wo_codes[:, g, :].bitcast(FP8X4),
+                scales=wo_scales[:, g, :],
+                in_=grouped[:].rearrange("p w n t -> p (w n t)"),
+            )
+
+        h_sb = keep.tile([P, M_TILES, E], F32)
+        sumsq = keep.tile([P, M_TILES], F32)
+        for m in range(M_TILES):
+            for n in range(E // N_TILE):
+                cols = slice(n * N_TILE, (n + 1) * N_TILE)
+                acc = psum.tile([P, N_TILE], F32, tag="bank", name="acc")
+                for g in range(PASSES):
+                    nc.tensor.matmul_mx(
+                        out=acc[:],
+                        lhsT=a_codes[:, m, g, :].bitcast(FP8X4),
+                        lhsT_scale=a_scales[:, m, g, :],
+                        rhs=wo_codes[:, g, cols].bitcast(FP8X4),
+                        rhs_scale=wo_scales[:, g, cols],
+                        start=(g == 0),
+                        stop=(g == PASSES - 1),
+                    )
+                nc.vector.tensor_tensor(out=h_sb[:, m, cols], in0=acc[:], in1=x_sb[:, m, cols], op=ALU.add)
+            nc.sync.dma_start(out=h_rows[m * P : (m + 1) * P, :], in_=h_sb[:, m, :])
+            squares = work.tile([P, E], BF16, tag="squares", name="squares")
+            nc.scalar.activation(out=squares[:], in_=h_sb[:, m, :], func=ACT.Square, accum_out=sumsq[:, m : m + 1])
+
+        std = keep.tile([P, M_TILES], F32)
+        nc.scalar.activation(out=std[:], in_=sumsq[:], func=ACT.Sqrt, scale=1.0 / E, bias=eps[:, 0:1])
+        rstd = keep.tile([P, M_TILES], F32)
+        nc.vector.reciprocal(out=rstd[:], in_=std[:])
+
+        h_grouped = keep.tile([P, M_TILES, PASSES, P, PACK], BF16, align_bytes=64)
+        hn_codes = keep.tile([P, M_TILES, PASSES, P], U32, align_bytes=64)
+        hn_scales = keep.tile([P, M_TILES, PASSES, P], U8, align_bytes=64)
+        for m in range(M_TILES):
+            hn = work.tile([P, E], BF16, tag="hn", name="hn")
+            nc.vector.scalar_tensor_tensor(
+                out=hn[:], in0=h_sb[:, m, :], scalar=rstd[:, m : m + 1], in1=gain[:], op0=ALU.mult, op1=ALU.mult
+            )
+            hn_t = psum.tile([P, PASSES, PACK, P], BF16, tag="bank", name="hn_t")
+            for g in range(PASSES):
+                for t in range(PACK):
+                    e0 = g * K_PASS + t * P
+                    nc.tensor.transpose(hn_t[:, g, t, :], hn[:, e0 : e0 + P], ident_bf16[:])
+            nc.scalar.copy(out=h_grouped[:, m], in_=hn_t[:].rearrange("p g t r -> p g r t"))
+            nc.vector.quantize_mx(
+                out=hn_codes[:, m].rearrange("p g r -> p (g r)").bitcast(FP8X4),
+                scales=hn_scales[:, m].rearrange("p g r -> p (g r)"),
+                in_=h_grouped[:, m].rearrange("p g r t -> p (g r t)"),
+            )
+
+        for q in range(F // LOAD_COLS):
+            load_cols = slice(q * LOAD_COLS, (q + 1) * LOAD_COLS)
+            gate_raw = []
+            up_raw = []
+            for g in range(PASSES):
+                raw_g = raw_pool.tile([P, PACK, LOAD_COLS], BF16, tag="raw", name="raw_g")
+                nc.sync.dma_start(out=raw_g[:], in_=gate_rows[g][:, :, load_cols])
+                gate_raw.append(raw_g)
+                raw_u = raw_pool.tile([P, PACK, LOAD_COLS], BF16, tag="raw", name="raw_u")
+                nc.sync.dma_start(out=raw_u[:], in_=up_rows[g][:, :, load_cols])
+                up_raw.append(raw_u)
+            for c in range(LOAD_COLS // N_TILE):
+                cols = slice(c * N_TILE, (c + 1) * N_TILE)
+                w_codes = code_pool.tile([P, PASSES, 2, N_TILE], U32, align_bytes=64, tag="w_codes", name="w_codes")
+                w_scales = code_pool.tile([P, PASSES, 2, N_TILE], U8, align_bytes=64, tag="w_scales", name="w_scales")
+                for g in range(PASSES):
+                    grouped = stage.tile([P, 2, N_TILE, PACK], BF16, align_bytes=64, tag="grouped", name="grouped")
+                    regroup(nc.vector.tensor_copy, grouped[:, 0], gate_raw[g][:, :, cols])
+                    regroup(nc.scalar.copy, grouped[:, 1], up_raw[g][:, :, cols])
+                    nc.vector.quantize_mx(
+                        out=w_codes[:, g].rearrange("p w n -> p (w n)").bitcast(FP8X4),
+                        scales=w_scales[:, g].rearrange("p w n -> p (w n)"),
+                        in_=grouped[:].rearrange("p w n t -> p (w n t)"),
+                    )
+                f0 = q * LOAD_COLS + c * N_TILE
+                for m in range(M_TILES):
+                    banks = []
+                    for w in range(2):
+                        acc = psum.tile([P, N_TILE], F32, tag="bank", name="acc")
+                        for g in range(PASSES):
+                            nc.tensor.matmul_mx(
+                                out=acc[:],
+                                lhsT=hn_codes[:, m, g, :].bitcast(FP8X4),
+                                lhsT_scale=hn_scales[:, m, g, :],
+                                rhs=w_codes[:, g, w, :].bitcast(FP8X4),
+                                rhs_scale=w_scales[:, g, w, :],
+                                start=(g == 0),
+                                stop=(g == PASSES - 1),
+                            )
+                        banks.append(acc)
+                    gelu = work.tile([P, N_TILE], F32, tag="gelu", name="gelu")
+                    nc.scalar.activation(out=gelu[:], in_=banks[0][:], func=ACT.Gelu_apprx_tanh)
+                    product = work.tile([P, N_TILE], F32, tag="product", name="product")
+                    nc.vector.tensor_tensor(out=product[:], in0=banks[1][:], in1=gelu[:], op=ALU.mult)
+                    nc.sync.dma_start(out=act_rows[m * P : (m + 1) * P, f0 : f0 + N_TILE], in_=product[:])

@@ -22,6 +22,11 @@ PASSES = E // K_PASS
 N_TILE = 512
 LOAD_COLS = 1024
 EPS = 1e-6
+CHUNKS = F // N_TILE
+UNITS = CHUNKS * PASSES
+PAIRS = CHUNKS * M_TILES // 2
+LOADS = 2 * PASSES * (F // LOAD_COLS)
+RAW_BUFS = 8
 
 FLOPS = 2 * TOKENS * E * (E + 2 * F)
 
@@ -46,11 +51,48 @@ def tile_block_pb_kernel(tc, attn, x, w_out, scale2, w_gate, w_up, out_0, out_1)
     with ExitStack() as ctx:
         const = ctx.enter_context(tc.tile_pool(name="const", bufs=1))
         keep = ctx.enter_context(tc.tile_pool(name="keep", bufs=1))
-        raw_pool = ctx.enter_context(tc.tile_pool(name="raw", bufs=8))
+        raw_pool = ctx.enter_context(tc.tile_pool(name="raw", bufs=RAW_BUFS))
         stage = ctx.enter_context(tc.tile_pool(name="stage", bufs=3))
         code_pool = ctx.enter_context(tc.tile_pool(name="codes", bufs=3))
-        work = ctx.enter_context(tc.tile_pool(name="work", bufs=3))
+        work = ctx.enter_context(tc.tile_pool(name="work", bufs=4))
         psum = ctx.enter_context(tc.psum_pool(name="psum", bufs=8))
+        ctx.enter_context(tc.manual_schedule())
+
+        raw_of = {}
+        grouped_of = {}
+        codes_of = {}
+        banks_of = {}
+        gelu_of = {}
+
+        def load_weights(k):
+            q, rest = divmod(k, 2 * PASSES)
+            g, w = divmod(rest, 2)
+            rows = (gate_rows, up_rows)[w]
+            raw = raw_pool.tile([P, PACK, LOAD_COLS], BF16, tag="raw", name="raw_w")
+            nc.sync.dma_start(out=raw[:], in_=rows[g][:, :, q * LOAD_COLS : (q + 1) * LOAD_COLS])
+            raw_of[(w, g, q)] = raw
+
+        def regroup_unit(i):
+            j, g = divmod(i, PASSES)
+            q, c = divmod(j, LOAD_COLS // N_TILE)
+            cols = slice(c * N_TILE, (c + 1) * N_TILE)
+            grouped = stage.tile([P, 2, N_TILE, PACK], BF16, align_bytes=64, tag="grouped", name="grouped")
+            regroup(nc.vector.tensor_copy, grouped[:, 0], raw_of[(0, g, q)][:, :, cols])
+            regroup(nc.scalar.copy, grouped[:, 1], raw_of[(1, g, q)][:, :, cols])
+            grouped_of[i] = grouped
+
+        def quantise_unit(i):
+            j, g = divmod(i, PASSES)
+            if g == 0:
+                w_codes = code_pool.tile([P, PASSES, 2, N_TILE], U32, align_bytes=64, tag="w_codes", name="w_codes")
+                w_scales = code_pool.tile([P, PASSES, 2, N_TILE], U8, align_bytes=64, tag="w_scales", name="w_scales")
+                codes_of[j] = (w_codes, w_scales)
+            w_codes, w_scales = codes_of[j]
+            nc.vector.quantize_mx(
+                out=w_codes[:, g].rearrange("p w n -> p (w n)").bitcast(FP8X4),
+                scales=w_scales[:, g].rearrange("p w n -> p (w n)"),
+                in_=grouped_of[i][:].rearrange("p w n t -> p (w n t)"),
+            )
 
         ident_f32 = const.tile([P, P], F32)
         make_identity(nc, ident_f32[:])
@@ -62,11 +104,9 @@ def tile_block_pb_kernel(tc, attn, x, w_out, scale2, w_gate, w_up, out_0, out_1)
         nc.vector.memset(eps[:], EPS)
         gain_row = const.tile([P, E], BF16)
         nc.vector.memset(gain_row[:], 0.0)
-        nc.scalar.dma_start(out=gain_row[0:1, :], in_=scale2.unsqueeze(0))
+        warm = const.tile([P, 1], F32)
+        nc.scalar.activation(out=warm[:], in_=eps[:], func=ACT.Sqrt)
 
-        a_sb = keep.tile([P, M_TILES, E], BF16)
-        for m in range(M_TILES):
-            nc.sync.dma_start(out=a_sb[:, m, :], in_=attn_rows[m * P : (m + 1) * P, :])
         w_out_raw = []
         for g in range(PASSES):
             raw = raw_pool.tile([P, PACK, LOAD_COLS], BF16, tag="raw", name="raw_o")
@@ -77,15 +117,29 @@ def tile_block_pb_kernel(tc, attn, x, w_out, scale2, w_gate, w_up, out_0, out_1)
                     in_=w_out_rows[first : first + 2 * P, :].rearrange("(p e) n -> p e n", e=2),
                 )
             w_out_raw.append(raw)
+        a_sb = keep.tile([P, M_TILES, E], BF16)
+        for m in range(M_TILES):
+            nc.sync.dma_start(out=a_sb[:, m, :], in_=attn_rows[m * P : (m + 1) * P, :])
+        nc.sync.dma_start(out=gain_row[0:1, :], in_=scale2.unsqueeze(0))
         x_sb = keep.tile([P, M_TILES, E], BF16)
-        nc.sync.dma_start(out=x_sb[:], in_=x_rows.rearrange("(m p) e -> p m e", p=P))
+        for m in range(M_TILES):
+            nc.sync.dma_start(out=x_sb[:, m, :], in_=x_rows[m * P : (m + 1) * P, :])
+        for k in range(RAW_BUFS - PASSES):
+            load_weights(k)
 
-        gain = const.tile([P, E], F32)
-        for n in range(E // N_TILE):
-            cols = slice(n * N_TILE, (n + 1) * N_TILE)
-            spread = psum.tile([P, N_TILE], F32, tag="bank", name="spread")
-            nc.tensor.matmul(out=spread[:], lhsT=ones[:], rhs=gain_row[:, cols], start=True, stop=True)
-            nc.scalar.copy(out=gain[:, cols], in_=spread[:])
+        wo_codes = keep.tile([P, PASSES, E], U32, align_bytes=64)
+        wo_scales = keep.tile([P, PASSES, E], U8, align_bytes=64)
+        for g in range(PASSES):
+            grouped = stage.tile([P, 2, N_TILE, PACK], BF16, align_bytes=64, tag="grouped", name="grouped")
+            regroup(nc.vector.tensor_copy, grouped[:, 0], w_out_raw[g][:, :, 0:N_TILE])
+            regroup(nc.scalar.copy, grouped[:, 1], w_out_raw[g][:, :, N_TILE : 2 * N_TILE])
+            nc.vector.quantize_mx(
+                out=wo_codes[:, g, :].bitcast(FP8X4),
+                scales=wo_scales[:, g, :],
+                in_=grouped[:].rearrange("p w n t -> p (w n t)"),
+            )
+        for k in range(RAW_BUFS - PASSES, RAW_BUFS):
+            load_weights(k)
 
         a_grouped = keep.tile([P, M_TILES, PASSES * P * PACK], BF16, align_bytes=64)
         a_codes = keep.tile([P, M_TILES, PASSES, P], U32, align_bytes=64)
@@ -101,23 +155,19 @@ def tile_block_pb_kernel(tc, attn, x, w_out, scale2, w_gate, w_up, out_0, out_1)
                 out=a_grouped[:, m, :].bitcast(F32).rearrange("p (g r u) -> p g r u", g=PASSES, u=2),
                 in_=a_t[:].rearrange("p g u r -> p g r u"),
             )
+        for m in range(M_TILES):
             nc.vector.quantize_mx(
                 out=a_codes[:, m].rearrange("p g r -> p (g r)").bitcast(FP8X4),
                 scales=a_scales[:, m].rearrange("p g r -> p (g r)"),
                 in_=a_grouped[:, m, :],
             )
 
-        wo_codes = keep.tile([P, PASSES, E], U32, align_bytes=64)
-        wo_scales = keep.tile([P, PASSES, E], U8, align_bytes=64)
-        for g in range(PASSES):
-            grouped = stage.tile([P, 2, N_TILE, PACK], BF16, align_bytes=64, tag="grouped", name="grouped")
-            regroup(nc.vector.tensor_copy, grouped[:, 0], w_out_raw[g][:, :, 0:N_TILE])
-            regroup(nc.scalar.copy, grouped[:, 1], w_out_raw[g][:, :, N_TILE : 2 * N_TILE])
-            nc.vector.quantize_mx(
-                out=wo_codes[:, g, :].bitcast(FP8X4),
-                scales=wo_scales[:, g, :],
-                in_=grouped[:].rearrange("p w n t -> p (w n t)"),
-            )
+        gain = const.tile([P, E], F32)
+        for n in range(E // N_TILE):
+            cols = slice(n * N_TILE, (n + 1) * N_TILE)
+            spread = psum.tile([P, N_TILE], F32, tag="bank", name="spread")
+            nc.tensor.matmul(out=spread[:], lhsT=ones[:], rhs=gain_row[:, cols], start=True, stop=True)
+            nc.scalar.copy(out=gain[:, cols], in_=spread[:])
 
         h_sb = keep.tile([P, M_TILES, E], F32)
         sumsq = keep.tile([P, M_TILES], F32)
@@ -142,6 +192,7 @@ def tile_block_pb_kernel(tc, attn, x, w_out, scale2, w_gate, w_up, out_0, out_1)
 
         std = keep.tile([P, M_TILES], F32)
         nc.scalar.activation(out=std[:], in_=sumsq[:], func=ACT.Sqrt, scale=1.0 / E, bias=eps[:, 0:1])
+        regroup_unit(0)
         rstd = keep.tile([P, M_TILES], F32)
         nc.vector.reciprocal(out=rstd[:], in_=std[:])
 
@@ -159,54 +210,60 @@ def tile_block_pb_kernel(tc, attn, x, w_out, scale2, w_gate, w_up, out_0, out_1)
                     e0 = g * K_PASS + t * P
                     nc.tensor.transpose(hn_t[:, g, t, :], hn[:, e0 : e0 + P], ident_bf16[:])
             nc.scalar.copy(out=h_grouped[:, m], in_=hn_t[:].rearrange("p g t r -> p g r t"))
+        regroup_unit(1)
+        quantise_unit(0)
+        for m in range(M_TILES):
             nc.vector.quantize_mx(
                 out=hn_codes[:, m].rearrange("p g r -> p (g r)").bitcast(FP8X4),
                 scales=hn_scales[:, m].rearrange("p g r -> p (g r)"),
                 in_=h_grouped[:, m].rearrange("p g r t -> p (g r t)"),
             )
 
-        for q in range(F // LOAD_COLS):
-            load_cols = slice(q * LOAD_COLS, (q + 1) * LOAD_COLS)
-            gate_raw = []
-            up_raw = []
+        def token_tiles(r):
+            j, half = divmod(r, 2)
+            return [(j, 2 * half), (j, 2 * half + 1)]
+
+        def multiply_pair(r):
+            for j, m in token_tiles(r):
+                acc_gate = psum.tile([P, N_TILE], F32, tag="bank", name="acc_gate")
+                acc_up = psum.tile([P, N_TILE], F32, tag="bank", name="acc_up")
+                banks_of[(j, m)] = (acc_gate, acc_up)
             for g in range(PASSES):
-                raw_g = raw_pool.tile([P, PACK, LOAD_COLS], BF16, tag="raw", name="raw_g")
-                nc.sync.dma_start(out=raw_g[:], in_=gate_rows[g][:, :, load_cols])
-                gate_raw.append(raw_g)
-                raw_u = raw_pool.tile([P, PACK, LOAD_COLS], BF16, tag="raw", name="raw_u")
-                nc.sync.dma_start(out=raw_u[:], in_=up_rows[g][:, :, load_cols])
-                up_raw.append(raw_u)
-            for c in range(LOAD_COLS // N_TILE):
-                cols = slice(c * N_TILE, (c + 1) * N_TILE)
-                w_codes = code_pool.tile([P, PASSES, 2, N_TILE], U32, align_bytes=64, tag="w_codes", name="w_codes")
-                w_scales = code_pool.tile([P, PASSES, 2, N_TILE], U8, align_bytes=64, tag="w_scales", name="w_scales")
-                for g in range(PASSES):
-                    grouped = stage.tile([P, 2, N_TILE, PACK], BF16, align_bytes=64, tag="grouped", name="grouped")
-                    regroup(nc.vector.tensor_copy, grouped[:, 0], gate_raw[g][:, :, cols])
-                    regroup(nc.scalar.copy, grouped[:, 1], up_raw[g][:, :, cols])
-                    nc.vector.quantize_mx(
-                        out=w_codes[:, g].rearrange("p w n -> p (w n)").bitcast(FP8X4),
-                        scales=w_scales[:, g].rearrange("p w n -> p (w n)"),
-                        in_=grouped[:].rearrange("p w n t -> p (w n t)"),
-                    )
-                f0 = q * LOAD_COLS + c * N_TILE
-                for m in range(M_TILES):
-                    banks = []
+                for j, m in token_tiles(r):
+                    w_codes, w_scales = codes_of[j]
                     for w in range(2):
-                        acc = psum.tile([P, N_TILE], F32, tag="bank", name="acc")
-                        for g in range(PASSES):
-                            nc.tensor.matmul_mx(
-                                out=acc[:],
-                                lhsT=hn_codes[:, m, g, :].bitcast(FP8X4),
-                                lhsT_scale=hn_scales[:, m, g, :],
-                                rhs=w_codes[:, g, w, :].bitcast(FP8X4),
-                                rhs_scale=w_scales[:, g, w, :],
-                                start=(g == 0),
-                                stop=(g == PASSES - 1),
-                            )
-                        banks.append(acc)
-                    gelu = work.tile([P, N_TILE], F32, tag="gelu", name="gelu")
-                    nc.scalar.activation(out=gelu[:], in_=banks[0][:], func=ACT.Gelu_apprx_tanh)
-                    product = work.tile([P, N_TILE], F32, tag="product", name="product")
-                    nc.vector.tensor_tensor(out=product[:], in0=banks[1][:], in1=gelu[:], op=ALU.mult)
-                    nc.sync.dma_start(out=act_rows[m * P : (m + 1) * P, f0 : f0 + N_TILE], in_=product[:])
+                        nc.tensor.matmul_mx(
+                            out=banks_of[(j, m)][w][:],
+                            lhsT=hn_codes[:, m, g, :].bitcast(FP8X4),
+                            lhsT_scale=hn_scales[:, m, g, :],
+                            rhs=w_codes[:, g, w, :].bitcast(FP8X4),
+                            rhs_scale=w_scales[:, g, w, :],
+                            start=(g == 0),
+                            stop=(g == PASSES - 1),
+                        )
+
+        def gelu_of_gate(j, m):
+            gelu = work.tile([P, N_TILE], F32, tag="gelu", name="gelu")
+            nc.scalar.activation(out=gelu[:], in_=banks_of[(j, m)][0][:], func=ACT.Gelu_apprx_tanh)
+            gelu_of[(j, m)] = gelu
+
+        def product_and_store(j, m):
+            product = work.tile([P, N_TILE], F32, tag="product", name="product")
+            nc.vector.tensor_tensor(out=product[:], in0=banks_of[(j, m)][1][:], in1=gelu_of[(j, m)][:], op=ALU.mult)
+            nc.sync.dma_start(out=act_rows[m * P : (m + 1) * P, j * N_TILE : (j + 1) * N_TILE], in_=product[:])
+
+        for i in range(2, UNITS + 4):
+            if 0 <= i - 4:
+                for j, m in token_tiles(i - 4):
+                    product_and_store(j, m)
+            if i < UNITS:
+                regroup_unit(i)
+            if i <= UNITS:
+                quantise_unit(i - 1)
+            if i + RAW_BUFS - 2 < LOADS:
+                load_weights(i + RAW_BUFS - 2)
+            if 0 <= i - 3 < PAIRS:
+                for j, m in token_tiles(i - 3):
+                    gelu_of_gate(j, m)
+            if i - 2 < PAIRS:
+                multiply_pair(i - 2)

@@ -27,6 +27,7 @@ UNITS = CHUNKS * PASSES
 PAIRS = CHUNKS * M_TILES // 2
 LOADS = 2 * PASSES * (F // LOAD_COLS)
 RAW_BUFS = 8
+PRODUCT_BUFS = 8
 
 FLOPS = 2 * TOKENS * E * (E + 2 * F)
 
@@ -186,8 +187,7 @@ def tile_block_pb_kernel(tc, attn, x, w_out, scale2, w_gate, w_up, out_0, out_1)
                         stop=(g == PASSES - 1),
                     )
                 nc.vector.tensor_tensor(out=h_sb[:, m, cols], in0=acc[:], in1=x_sb[:, m, cols], op=ALU.add)
-            nc.sync.dma_start(out=h_rows[m * P : (m + 1) * P, :], in_=h_sb[:, m, :])
-            squares = work.tile([P, E], BF16, tag="squares", name="squares")
+            squares = work.tile([P, E], BF16, tag="squares", name="squares", bufs=2)
             nc.scalar.activation(out=squares[:], in_=h_sb[:, m, :], func=ACT.Square, accum_out=sumsq[:, m : m + 1])
 
         std = keep.tile([P, M_TILES], F32)
@@ -200,7 +200,7 @@ def tile_block_pb_kernel(tc, attn, x, w_out, scale2, w_gate, w_up, out_0, out_1)
         hn_codes = keep.tile([P, M_TILES, PASSES, P], U32, align_bytes=64)
         hn_scales = keep.tile([P, M_TILES, PASSES, P], U8, align_bytes=64)
         for m in range(M_TILES):
-            hn = work.tile([P, E], BF16, tag="hn", name="hn")
+            hn = work.tile([P, E], BF16, tag="hn", name="hn", bufs=2)
             nc.vector.scalar_tensor_tensor(
                 out=hn[:], in0=h_sb[:, m, :], scalar=rstd[:, m : m + 1], in1=gain[:], op0=ALU.mult, op1=ALU.mult
             )
@@ -248,7 +248,7 @@ def tile_block_pb_kernel(tc, attn, x, w_out, scale2, w_gate, w_up, out_0, out_1)
             gelu_of[(j, m)] = gelu
 
         def product_and_store(j, m):
-            product = work.tile([P, N_TILE], F32, tag="product", name="product")
+            product = work.tile([P, N_TILE], F32, tag="product", name="product", bufs=PRODUCT_BUFS)
             nc.vector.tensor_tensor(out=product[:], in0=banks_of[(j, m)][1][:], in1=gelu_of[(j, m)][:], op=ALU.mult)
             nc.sync.dma_start(out=act_rows[m * P : (m + 1) * P, j * N_TILE : (j + 1) * N_TILE], in_=product[:])
 
@@ -260,8 +260,12 @@ def tile_block_pb_kernel(tc, attn, x, w_out, scale2, w_gate, w_up, out_0, out_1)
                 regroup_unit(i)
             if i <= UNITS:
                 quantise_unit(i - 1)
-            if i + RAW_BUFS - 2 < LOADS:
-                load_weights(i + RAW_BUFS - 2)
+            k = i + RAW_BUFS - 2
+            if k < LOADS:
+                load_weights(k)
+            elif k - LOADS < M_TILES:
+                m = k - LOADS
+                nc.sync.dma_start(out=h_rows[m * P : (m + 1) * P, :], in_=h_sb[:, m, :])
             if 0 <= i - 3 < PAIRS:
                 for j, m in token_tiles(i - 3):
                     gelu_of_gate(j, m)

@@ -27,7 +27,7 @@ UNITS = CHUNKS * PASSES
 PAIRS = CHUNKS * M_TILES // 2
 LOADS = 2 * PASSES * (F // LOAD_COLS)
 RAW_BUFS = 8
-PRODUCT_BUFS = 8
+BANK_TAGS = ("gate", "up")
 
 FLOPS = 2 * TOKENS * E * (E + 2 * F)
 
@@ -56,14 +56,14 @@ def tile_block_pb_kernel(tc, attn, x, w_out, scale2, w_gate, w_up, out_0, out_1)
         stage = ctx.enter_context(tc.tile_pool(name="stage", bufs=3))
         code_pool = ctx.enter_context(tc.tile_pool(name="codes", bufs=3))
         work = ctx.enter_context(tc.tile_pool(name="work", bufs=4))
-        psum = ctx.enter_context(tc.psum_pool(name="psum", bufs=8))
+        psum = ctx.enter_context(tc.psum_pool(name="psum", bufs=4))
         ctx.enter_context(tc.manual_schedule())
 
         raw_of = {}
         grouped_of = {}
         codes_of = {}
         banks_of = {}
-        gelu_of = {}
+        gated_of = {}
 
         def load_weights(k):
             q, rest = divmod(k, 2 * PASSES)
@@ -147,7 +147,7 @@ def tile_block_pb_kernel(tc, attn, x, w_out, scale2, w_gate, w_up, out_0, out_1)
         a_scales = keep.tile([P, M_TILES, PASSES, P], U8, align_bytes=64)
         for m in range(M_TILES):
             a_words = a_sb[:, m, :].bitcast(F32)
-            a_t = psum.tile([P, PASSES, 2, P], F32, tag="bank", name="a_t")
+            a_t = psum.tile([P, PASSES, 2, P], F32, tag=BANK_TAGS[m % 2], name="a_t")
             for g in range(PASSES):
                 for u in range(2):
                     w0 = (2 * g + u) * P
@@ -166,7 +166,7 @@ def tile_block_pb_kernel(tc, attn, x, w_out, scale2, w_gate, w_up, out_0, out_1)
         gain = const.tile([P, E], F32)
         for n in range(E // N_TILE):
             cols = slice(n * N_TILE, (n + 1) * N_TILE)
-            spread = psum.tile([P, N_TILE], F32, tag="bank", name="spread")
+            spread = psum.tile([P, N_TILE], F32, tag=BANK_TAGS[n], name="spread")
             nc.tensor.matmul(out=spread[:], lhsT=ones[:], rhs=gain_row[:, cols], start=True, stop=True)
             nc.scalar.copy(out=gain[:, cols], in_=spread[:])
 
@@ -175,7 +175,7 @@ def tile_block_pb_kernel(tc, attn, x, w_out, scale2, w_gate, w_up, out_0, out_1)
         for m in range(M_TILES):
             for n in range(E // N_TILE):
                 cols = slice(n * N_TILE, (n + 1) * N_TILE)
-                acc = psum.tile([P, N_TILE], F32, tag="bank", name="acc")
+                acc = psum.tile([P, N_TILE], F32, tag=BANK_TAGS[n], name="acc")
                 for g in range(PASSES):
                     nc.tensor.matmul_mx(
                         out=acc[:],
@@ -187,7 +187,8 @@ def tile_block_pb_kernel(tc, attn, x, w_out, scale2, w_gate, w_up, out_0, out_1)
                         stop=(g == PASSES - 1),
                     )
                 nc.vector.tensor_tensor(out=h_sb[:, m, cols], in0=acc[:], in1=x_sb[:, m, cols], op=ALU.add)
-            squares = work.tile([P, E], BF16, tag="squares", name="squares", bufs=2)
+            nc.sync.dma_start(out=h_rows[m * P : (m + 1) * P, :], in_=h_sb[:, m, :])
+            squares = work.tile([P, E], BF16, tag="squares", name="squares")
             nc.scalar.activation(out=squares[:], in_=h_sb[:, m, :], func=ACT.Square, accum_out=sumsq[:, m : m + 1])
 
         std = keep.tile([P, M_TILES], F32)
@@ -200,11 +201,11 @@ def tile_block_pb_kernel(tc, attn, x, w_out, scale2, w_gate, w_up, out_0, out_1)
         hn_codes = keep.tile([P, M_TILES, PASSES, P], U32, align_bytes=64)
         hn_scales = keep.tile([P, M_TILES, PASSES, P], U8, align_bytes=64)
         for m in range(M_TILES):
-            hn = work.tile([P, E], BF16, tag="hn", name="hn", bufs=2)
+            hn = work.tile([P, E], BF16, tag="hn", name="hn")
             nc.vector.scalar_tensor_tensor(
                 out=hn[:], in0=h_sb[:, m, :], scalar=rstd[:, m : m + 1], in1=gain[:], op0=ALU.mult, op1=ALU.mult
             )
-            hn_t = psum.tile([P, PASSES, PACK, P], BF16, tag="bank", name="hn_t")
+            hn_t = psum.tile([P, PASSES, PACK, P], BF16, tag=BANK_TAGS[m % 2], name="hn_t")
             for g in range(PASSES):
                 for t in range(PACK):
                     e0 = g * K_PASS + t * P
@@ -225,13 +226,13 @@ def tile_block_pb_kernel(tc, attn, x, w_out, scale2, w_gate, w_up, out_0, out_1)
 
         def multiply_pair(r):
             for j, m in token_tiles(r):
-                acc_gate = psum.tile([P, N_TILE], F32, tag="bank", name="acc_gate")
-                acc_up = psum.tile([P, N_TILE], F32, tag="bank", name="acc_up")
+                acc_gate = psum.tile([P, N_TILE], F32, tag="gate", name="acc_gate")
+                acc_up = psum.tile([P, N_TILE], F32, tag="up", name="acc_up")
                 banks_of[(j, m)] = (acc_gate, acc_up)
-            for g in range(PASSES):
+            for w in range(2):
                 for j, m in token_tiles(r):
                     w_codes, w_scales = codes_of[j]
-                    for w in range(2):
+                    for g in range(PASSES):
                         nc.tensor.matmul_mx(
                             out=banks_of[(j, m)][w][:],
                             lhsT=hn_codes[:, m, g, :].bitcast(FP8X4),
@@ -242,32 +243,32 @@ def tile_block_pb_kernel(tc, attn, x, w_out, scale2, w_gate, w_up, out_0, out_1)
                             stop=(g == PASSES - 1),
                         )
 
-        def gelu_of_gate(j, m):
-            gelu = work.tile([P, N_TILE], F32, tag="gelu", name="gelu")
-            nc.scalar.activation(out=gelu[:], in_=banks_of[(j, m)][0][:], func=ACT.Gelu_apprx_tanh)
-            gelu_of[(j, m)] = gelu
+        def gelu_pair(r):
+            gated = work.tile([P, 2, N_TILE], F32, tag="gated", name="gated")
+            for half, (j, m) in enumerate(token_tiles(r)):
+                nc.scalar.activation(out=gated[:, half, :], in_=banks_of[(j, m)][0][:], func=ACT.Gelu_apprx_tanh)
+            gated_of[r] = gated
 
-        def product_and_store(j, m):
-            product = work.tile([P, N_TILE], F32, tag="product", name="product", bufs=PRODUCT_BUFS)
-            nc.vector.tensor_tensor(out=product[:], in0=banks_of[(j, m)][1][:], in1=gelu_of[(j, m)][:], op=ALU.mult)
-            nc.sync.dma_start(out=act_rows[m * P : (m + 1) * P, j * N_TILE : (j + 1) * N_TILE], in_=product[:])
+        def product_pair(r):
+            gated = gated_of[r]
+            for half, (j, m) in reversed(list(enumerate(token_tiles(r)))):
+                nc.vector.tensor_tensor(
+                    out=gated[:, half, :], in0=banks_of[(j, m)][1][:], in1=gated[:, half, :], op=ALU.mult
+                )
+                nc.sync.dma_start(
+                    out=act_rows[m * P : (m + 1) * P, j * N_TILE : (j + 1) * N_TILE], in_=gated[:, half, :]
+                )
 
         for i in range(2, UNITS + 4):
-            if 0 <= i - 4:
-                for j, m in token_tiles(i - 4):
-                    product_and_store(j, m)
             if i < UNITS:
                 regroup_unit(i)
             if i <= UNITS:
                 quantise_unit(i - 1)
-            k = i + RAW_BUFS - 2
-            if k < LOADS:
-                load_weights(k)
-            elif k - LOADS < M_TILES:
-                m = k - LOADS
-                nc.sync.dma_start(out=h_rows[m * P : (m + 1) * P, :], in_=h_sb[:, m, :])
-            if 0 <= i - 3 < PAIRS:
-                for j, m in token_tiles(i - 3):
-                    gelu_of_gate(j, m)
+            if i + RAW_BUFS - 2 < LOADS:
+                load_weights(i + RAW_BUFS - 2)
+            if 0 <= i - 4:
+                product_pair(i - 4)
             if i - 2 < PAIRS:
                 multiply_pair(i - 2)
+            if 0 <= i - 3 < PAIRS:
+                gelu_pair(i - 3)

from contextlib import ExitStack

import concourse.mybir as mybir
from concourse.masks import make_identity

F32 = mybir.dt.float32
BF16 = mybir.dt.bfloat16
U32 = mybir.dt.uint32
U8 = mybir.dt.uint8
FP8X4 = mybir.dt.float8_e4m3fn_x4
ACT = mybir.ActivationFunctionType
ALU = mybir.AluOpType

P = 128
PACK = 4
K_PASS = P * PACK
TOKENS = 512
E = 1024
F = 4096
M_TILES = TOKENS // P
PASSES = E // K_PASS
N_TILE = 512
LOAD_COLS = 1024
EPS = 1e-6
CHUNKS = F // N_TILE
UNITS = CHUNKS * PASSES
PAIRS = CHUNKS * M_TILES // 2
LOADS = 2 * PASSES * (F // LOAD_COLS)
RAW_BUFS = 8
BANK_TAGS = ("gate", "up")

FLOPS = 2 * TOKENS * E * (E + 2 * F)


def regroup(copy, grouped, rows):
    copy(
        out=grouped.rearrange("p (c i) t -> p c t i", i=4),
        in_=rows.rearrange("p t (c i) -> p c t i", i=4),
    )


def tile_block_pb_kernel(tc, attn, x, w_out, scale2, w_gate, w_up, out_0, out_1):
    nc = tc.nc
    attn_rows = attn.rearrange("b s i d -> (b s) (i d)")
    x_rows = x.rearrange("b s e -> (b s) e")
    w_out_rows = w_out.rearrange("i d e -> (i d) e")
    h_rows = out_0.rearrange("b s e -> (b s) e")
    act_rows = out_1.rearrange("b s f -> (b s) f")
    gate_rows = w_gate.rearrange("(g t p) n -> g p t n", t=PACK, p=P)
    up_rows = w_up.rearrange("(g t p) n -> g p t n", t=PACK, p=P)

    with ExitStack() as ctx:
        const = ctx.enter_context(tc.tile_pool(name="const", bufs=1))
        keep = ctx.enter_context(tc.tile_pool(name="keep", bufs=1))
        raw_pool = ctx.enter_context(tc.tile_pool(name="raw", bufs=RAW_BUFS))
        stage = ctx.enter_context(tc.tile_pool(name="stage", bufs=3))
        code_pool = ctx.enter_context(tc.tile_pool(name="codes", bufs=3))
        work = ctx.enter_context(tc.tile_pool(name="work", bufs=4))
        psum = ctx.enter_context(tc.psum_pool(name="psum", bufs=4))
        ctx.enter_context(tc.manual_schedule())

        raw_of = {}
        grouped_of = {}
        codes_of = {}
        banks_of = {}
        gated_of = {}

        def load_weights(k):
            q, rest = divmod(k, 2 * PASSES)
            g, w = divmod(rest, 2)
            rows = (gate_rows, up_rows)[w]
            raw = raw_pool.tile([P, PACK, LOAD_COLS], BF16, tag="raw", name="raw_w")
            nc.sync.dma_start(out=raw[:], in_=rows[g][:, :, q * LOAD_COLS : (q + 1) * LOAD_COLS])
            raw_of[(w, g, q)] = raw

        def regroup_unit(i):
            j, g = divmod(i, PASSES)
            q, c = divmod(j, LOAD_COLS // N_TILE)
            cols = slice(c * N_TILE, (c + 1) * N_TILE)
            grouped = stage.tile([P, 2, N_TILE, PACK], BF16, align_bytes=64, tag="grouped", name="grouped")
            regroup(nc.vector.tensor_copy, grouped[:, 0], raw_of[(0, g, q)][:, :, cols])
            regroup(nc.scalar.copy, grouped[:, 1], raw_of[(1, g, q)][:, :, cols])
            grouped_of[i] = grouped

        def quantise_unit(i):
            j, g = divmod(i, PASSES)
            if g == 0:
                w_codes = code_pool.tile([P, PASSES, 2, N_TILE], U32, align_bytes=64, tag="w_codes", name="w_codes")
                w_scales = code_pool.tile([P, PASSES, 2, N_TILE], U8, align_bytes=64, tag="w_scales", name="w_scales")
                codes_of[j] = (w_codes, w_scales)
            w_codes, w_scales = codes_of[j]
            nc.vector.quantize_mx(
                out=w_codes[:, g].rearrange("p w n -> p (w n)").bitcast(FP8X4),
                scales=w_scales[:, g].rearrange("p w n -> p (w n)"),
                in_=grouped_of[i][:].rearrange("p w n t -> p (w n t)"),
            )

        ident_f32 = const.tile([P, P], F32)
        make_identity(nc, ident_f32[:])
        ident_bf16 = const.tile([P, P], BF16)
        make_identity(nc, ident_bf16[:])
        ones = const.tile([P, P], BF16)
        nc.vector.memset(ones[:], 1.0)
        eps = const.tile([P, 1], F32)
        nc.vector.memset(eps[:], EPS)
        gain_row = const.tile([P, E], BF16)
        nc.vector.memset(gain_row[:], 0.0)
        warm = const.tile([P, 1], F32)
        nc.scalar.activation(out=warm[:], in_=eps[:], func=ACT.Sqrt)

        w_out_raw = []
        for g in range(PASSES):
            raw = raw_pool.tile([P, PACK, LOAD_COLS], BF16, tag="raw", name="raw_o")
            for u in range(2):
                first = g * K_PASS + u * 2 * P
                nc.sync.dma_start(
                    out=raw[:, 2 * u : 2 * u + 2, :],
                    in_=w_out_rows[first : first + 2 * P, :].rearrange("(p e) n -> p e n", e=2),
                )
            w_out_raw.append(raw)
        a_sb = keep.tile([P, M_TILES, E], BF16)
        for m in range(M_TILES):
            nc.sync.dma_start(out=a_sb[:, m, :], in_=attn_rows[m * P : (m + 1) * P, :])
        nc.sync.dma_start(out=gain_row[0:1, :], in_=scale2.unsqueeze(0))
        x_sb = keep.tile([P, M_TILES, E], BF16)
        for m in range(M_TILES):
            nc.sync.dma_start(out=x_sb[:, m, :], in_=x_rows[m * P : (m + 1) * P, :])
        for k in range(RAW_BUFS - PASSES):
            load_weights(k)

        wo_codes = keep.tile([P, PASSES, E], U32, align_bytes=64)
        wo_scales = keep.tile([P, PASSES, E], U8, align_bytes=64)
        for g in range(PASSES):
            grouped = stage.tile([P, 2, N_TILE, PACK], BF16, align_bytes=64, tag="grouped", name="grouped")
            regroup(nc.vector.tensor_copy, grouped[:, 0], w_out_raw[g][:, :, 0:N_TILE])
            regroup(nc.scalar.copy, grouped[:, 1], w_out_raw[g][:, :, N_TILE : 2 * N_TILE])
            nc.vector.quantize_mx(
                out=wo_codes[:, g, :].bitcast(FP8X4),
                scales=wo_scales[:, g, :],
                in_=grouped[:].rearrange("p w n t -> p (w n t)"),
            )
        for k in range(RAW_BUFS - PASSES, RAW_BUFS):
            load_weights(k)

        a_grouped = keep.tile([P, M_TILES, PASSES * P * PACK], BF16, align_bytes=64)
        a_codes = keep.tile([P, M_TILES, PASSES, P], U32, align_bytes=64)
        a_scales = keep.tile([P, M_TILES, PASSES, P], U8, align_bytes=64)
        for m in range(M_TILES):
            a_words = a_sb[:, m, :].bitcast(F32)
            a_t = psum.tile([P, PASSES, 2, P], F32, tag=BANK_TAGS[m % 2], name="a_t")
            for g in range(PASSES):
                for u in range(2):
                    w0 = (2 * g + u) * P
                    nc.tensor.transpose(a_t[:, g, u, :], a_words[:, w0 : w0 + P], ident_f32[:])
            nc.scalar.copy(
                out=a_grouped[:, m, :].bitcast(F32).rearrange("p (g r u) -> p g r u", g=PASSES, u=2),
                in_=a_t[:].rearrange("p g u r -> p g r u"),
            )
        for m in range(M_TILES):
            nc.vector.quantize_mx(
                out=a_codes[:, m].rearrange("p g r -> p (g r)").bitcast(FP8X4),
                scales=a_scales[:, m].rearrange("p g r -> p (g r)"),
                in_=a_grouped[:, m, :],
            )

        gain = const.tile([P, E], F32)
        for n in range(E // N_TILE):
            cols = slice(n * N_TILE, (n + 1) * N_TILE)
            spread = psum.tile([P, N_TILE], F32, tag=BANK_TAGS[n], name="spread")
            nc.tensor.matmul(out=spread[:], lhsT=ones[:], rhs=gain_row[:, cols], start=True, stop=True)
            nc.scalar.copy(out=gain[:, cols], in_=spread[:])

        h_sb = keep.tile([P, M_TILES, E], F32)
        sumsq = keep.tile([P, M_TILES], F32)
        for m in range(M_TILES):
            for n in range(E // N_TILE):
                cols = slice(n * N_TILE, (n + 1) * N_TILE)
                acc = psum.tile([P, N_TILE], F32, tag=BANK_TAGS[n], name="acc")
                for g in range(PASSES):
                    nc.tensor.matmul_mx(
                        out=acc[:],
                        lhsT=a_codes[:, m, g, :].bitcast(FP8X4),
                        lhsT_scale=a_scales[:, m, g, :],
                        rhs=wo_codes[:, g, cols].bitcast(FP8X4),
                        rhs_scale=wo_scales[:, g, cols],
                        start=(g == 0),
                        stop=(g == PASSES - 1),
                    )
                nc.vector.tensor_tensor(out=h_sb[:, m, cols], in0=acc[:], in1=x_sb[:, m, cols], op=ALU.add)
            nc.sync.dma_start(out=h_rows[m * P : (m + 1) * P, :], in_=h_sb[:, m, :])
            squares = work.tile([P, E], BF16, tag="squares", name="squares")
            nc.scalar.activation(out=squares[:], in_=h_sb[:, m, :], func=ACT.Square, accum_out=sumsq[:, m : m + 1])

        std = keep.tile([P, M_TILES], F32)
        nc.scalar.activation(out=std[:], in_=sumsq[:], func=ACT.Sqrt, scale=1.0 / E, bias=eps[:, 0:1])
        regroup_unit(0)
        rstd = keep.tile([P, M_TILES], F32)
        nc.vector.reciprocal(out=rstd[:], in_=std[:])

        h_grouped = keep.tile([P, M_TILES, PASSES, P, PACK], BF16, align_bytes=64)
        hn_codes = keep.tile([P, M_TILES, PASSES, P], U32, align_bytes=64)
        hn_scales = keep.tile([P, M_TILES, PASSES, P], U8, align_bytes=64)
        for m in range(M_TILES):
            hn = work.tile([P, E], BF16, tag="hn", name="hn")
            nc.vector.scalar_tensor_tensor(
                out=hn[:], in0=h_sb[:, m, :], scalar=rstd[:, m : m + 1], in1=gain[:], op0=ALU.mult, op1=ALU.mult
            )
            hn_t = psum.tile([P, PASSES, PACK, P], BF16, tag=BANK_TAGS[m % 2], name="hn_t")
            for g in range(PASSES):
                for t in range(PACK):
                    e0 = g * K_PASS + t * P
                    nc.tensor.transpose(hn_t[:, g, t, :], hn[:, e0 : e0 + P], ident_bf16[:])
            nc.scalar.copy(out=h_grouped[:, m], in_=hn_t[:].rearrange("p g t r -> p g r t"))
        regroup_unit(1)
        quantise_unit(0)
        for m in range(M_TILES):
            nc.vector.quantize_mx(
                out=hn_codes[:, m].rearrange("p g r -> p (g r)").bitcast(FP8X4),
                scales=hn_scales[:, m].rearrange("p g r -> p (g r)"),
                in_=h_grouped[:, m].rearrange("p g r t -> p (g r t)"),
            )

        def token_tiles(r):
            j, half = divmod(r, 2)
            return [(j, 2 * half), (j, 2 * half + 1)]

        def multiply_pair(r):
            for j, m in token_tiles(r):
                acc_gate = psum.tile([P, N_TILE], F32, tag="gate", name="acc_gate")
                acc_up = psum.tile([P, N_TILE], F32, tag="up", name="acc_up")
                banks_of[(j, m)] = (acc_gate, acc_up)
            for w in range(2):
                for j, m in token_tiles(r):
                    w_codes, w_scales = codes_of[j]
                    for g in range(PASSES):
                        nc.tensor.matmul_mx(
                            out=banks_of[(j, m)][w][:],
                            lhsT=hn_codes[:, m, g, :].bitcast(FP8X4),
                            lhsT_scale=hn_scales[:, m, g, :],
                            rhs=w_codes[:, g, w, :].bitcast(FP8X4),
                            rhs_scale=w_scales[:, g, w, :],
                            start=(g == 0),
                            stop=(g == PASSES - 1),
                        )

        def gelu_pair(r):
            gated = work.tile([P, 2, N_TILE], F32, tag="gated", name="gated")
            for half, (j, m) in enumerate(token_tiles(r)):
                nc.scalar.activation(out=gated[:, half, :], in_=banks_of[(j, m)][0][:], func=ACT.Gelu_apprx_tanh)
            gated_of[r] = gated

        def product_pair(r):
            gated = gated_of[r]
            for half, (j, m) in reversed(list(enumerate(token_tiles(r)))):
                nc.vector.tensor_tensor(
                    out=gated[:, half, :], in0=banks_of[(j, m)][1][:], in1=gated[:, half, :], op=ALU.mult
                )
                nc.sync.dma_start(
                    out=act_rows[m * P : (m + 1) * P, j * N_TILE : (j + 1) * N_TILE], in_=gated[:, half, :]
                )

        for i in range(2, UNITS + 4):
            if i < UNITS:
                regroup_unit(i)
            if i <= UNITS:
                quantise_unit(i - 1)
            if i + RAW_BUFS - 2 < LOADS:
                load_weights(i + RAW_BUFS - 2)
            if 0 <= i - 4:
                product_pair(i - 4)
            if i - 2 < PAIRS:
                multiply_pair(i - 2)
            if 0 <= i - 3 < PAIRS:
                gelu_pair(i - 3)
